import numpy as np
import ml_dtypes


def mxq(x, axis, fmt="e4m3"):
    dtype, down = {"e4m3": (ml_dtypes.float8_e4m3fn, 7), "e5m2": (ml_dtypes.float8_e5m2, 14)}[fmt]
    v = np.moveaxis(np.asarray(x, np.float32).astype(ml_dtypes.bfloat16).astype(np.float64), axis, -1)
    blocks = v.reshape(v.shape[:-1] + (-1, 32))
    amax = np.abs(blocks).max(-1, keepdims=True)
    byte = np.maximum(np.where(amax > 0, np.frexp(amax)[1] - 1 + 127, 0) - down, 1)
    scale = np.exp2(byte - 127.0)
    codes = (blocks / scale).astype(np.float32).astype(dtype).astype(np.float64)
    return np.moveaxis((codes * scale).reshape(v.shape), -1, axis)


WIDE = False


def mx_kscale(k):
    if not WIDE:
        return np.ones(k)
    levels = np.array([10, -10, 5, -5, 0])
    a = np.random.permutation(np.resize(levels, k // 512 * 4)).reshape(k // 512, 4)
    idx = np.arange(k)
    return np.exp2(a[idx // 512, idx % 128 // 32])


BF16 = ml_dtypes.bfloat16


def bf(x):
    return np.asarray(x, np.float32).astype(BF16)


def f64(x):
    return np.asarray(x).astype(np.float64)


N, D_IN, UNITS = 1024, 1024, 1024


def setup_inputs():
    s = mx_kscale(D_IN)
    cu, cw = 0.6 / np.sqrt(D_IN), 0.6 / np.sqrt(UNITS)
    return {"X": bf(np.random.standard_normal((N, D_IN)) * s),
            "S": bf(np.random.standard_normal((N, UNITS))),
            "H": bf(np.tanh(np.random.standard_normal((N, UNITS)) * 0.8)),
            "Uz": bf(np.random.standard_normal((D_IN, UNITS)) * cu / s[:, None]),
            "Ug": bf(np.random.standard_normal((D_IN, UNITS)) * cu / s[:, None]),
            "Wz": bf(np.random.standard_normal((UNITS, UNITS)) * cw),
            "Wg": bf(np.random.standard_normal((UNITS, UNITS)) * cw),
            "bz": bf(np.random.standard_normal(UNITS) * 0.3),
            "bg": bf(np.random.standard_normal(UNITS) * 0.3)}


def reference(X, S, H, Uz, Ug, Wz, Wg, bz, bg):
    xq = mxq(f64(X), 1, "e4m3")
    Sf = f64(S)
    sq = mxq(Sf, 1, "e4m3")
    Z = np.tanh((xq @ mxq(f64(Uz), 0, "e4m3")) + (sq @ mxq(f64(Wz), 0, "e4m3")) + f64(bz))
    G = np.tanh((xq @ mxq(f64(Ug), 0, "e4m3")) + (sq @ mxq(f64(Wg), 0, "e4m3")) + f64(bg))
    return (1.0 - G) * f64(H) + Z * Sf

@@ -1,0 +1,244 @@
+from contextlib import ExitStack
+
+import concourse.mybir as mybir
+from concourse.masks import make_identity
+
+F32 = mybir.dt.float32
+BF16 = mybir.dt.bfloat16
+U32 = mybir.dt.uint32
+U8 = mybir.dt.uint8
+FP8X4 = mybir.dt.float8_e4m3fn_x4
+ALU = mybir.AluOpType
+TANH = mybir.ActivationFunctionType.Tanh
+
+P = 128
+PACK = 4
+K_PASS = P * PACK
+ROWS = 1024
+FEATURES = 1024
+UNITS = 1024
+PASSES = FEATURES // K_PASS
+PAIR = 2
+PAIRS = ROWS // (PAIR * P)
+HALF = 512
+HALVES = UNITS // HALF
+GATES = 2
+OPERANDS = 2
+BLOCKS = HALVES * GATES
+TILES_PER_BLOCK = OPERANDS * PASSES
+VECTOR_REGROUPS = 6
+
+FLOPS = 2 * ROWS * (OPERANDS * FEATURES) * (GATES * UNITS)
+
+
+def tile_lstmlayer_pb_kernel(tc, X, S, H, Uz, Ug, Wz, Wg, bz, bg, out):
+    nc = tc.nc
+    weights = ((Uz, Wz), (Ug, Wg))
+    biases = (bz, bg)
+
+    with ExitStack() as ctx:
+        const = ctx.enter_context(tc.tile_pool(name="const", bufs=1))
+        keep = ctx.enter_context(tc.tile_pool(name="keep", bufs=1))
+        w_in = ctx.enter_context(tc.tile_pool(name="w_in", bufs=2 * TILES_PER_BLOCK))
+        stage = ctx.enter_context(tc.tile_pool(name="stage", bufs=2))
+        w_mx = ctx.enter_context(tc.tile_pool(name="w_mx", bufs=2))
+        work = ctx.enter_context(tc.tile_pool(name="work", bufs=2))
+        psum = ctx.enter_context(tc.psum_pool(name="psum", bufs=8))
+
+        identity = const.tile([P, P], F32)
+        make_identity(nc, identity[:])
+        ones = const.tile([P, P], BF16)
+        nc.vector.memset(ones[:], 1.0)
+        warm = const.tile([P, 1], F32)
+        nc.vector.memset(warm[:], 0.0)
+        nc.scalar.activation(out=warm[:], in_=warm[:], func=TANH)
+        bias_rows = const.tile([P, GATES, UNITS], BF16)
+        nc.vector.memset(bias_rows[:], 0.0)
+
+        def row_pair(dram, pair):
+            rows = dram[pair * PAIR * P : (pair + 1) * PAIR * P, :]
+            return rows.rearrange("(i p) c -> p i c", p=P)
+
+        def load_rows(dram, pair, label):
+            loaded = keep.tile([P, PAIR, FEATURES], BF16, name="%s%d" % (label, pair))
+            nc.sync.dma_start(out=loaded[:], in_=row_pair(dram, pair))
+            return loaded
+
+        w_raw = {}
+
+        def load_weights(block):
+            half, gate = divmod(block, GATES)
+            for operand in range(OPERANDS):
+                for g in range(PASSES):
+                    raw = w_in.tile([P, PACK, HALF], BF16, tag="w_raw", name="w_raw")
+                    nc.sync.dma_start(
+                        out=raw[:],
+                        in_=weights[gate][operand][
+                            g * K_PASS : (g + 1) * K_PASS, half * HALF : (half + 1) * HALF
+                        ].rearrange("(p t) c -> p t c", t=PACK),
+                    )
+                    w_raw[(block * OPERANDS + operand) * PASSES + g] = raw
+
+        for gate in range(GATES):
+            nc.sync.dma_start(
+                out=bias_rows[0:1, gate, :], in_=biases[gate].rearrange("(o c) -> o c", o=1)
+            )
+        x_rows = [load_rows(X, 0, "x")]
+        s_rows = [load_rows(S, 0, "s")]
+        load_weights(0)
+        for pair in range(1, PAIRS):
+            x_rows.append(load_rows(X, pair, "x"))
+            s_rows.append(load_rows(S, pair, "s"))
+        load_weights(1)
+        h_rows = [load_rows(H, pair, "h") for pair in range(PAIRS)]
+
+        bias_all = const.tile([P, GATES, UNITS], F32)
+        for gate in range(GATES):
+            for half in range(HALVES):
+                cols = slice(half * HALF, (half + 1) * HALF)
+                spread = psum.tile([P, HALF], F32, tag="bank", name="spread")
+                nc.tensor.matmul(
+                    out=spread[:], lhsT=ones[:], rhs=bias_rows[:, gate, cols], start=True, stop=True
+                )
+                nc.scalar.copy(out=bias_all[:, gate, cols], in_=spread[:])
+
+        act_codes = keep.tile([P, OPERANDS, PAIRS * PAIR, PASSES, P], U32, align_bytes=64)
+        act_scales = keep.tile([P, OPERANDS, PAIRS * PAIR, PASSES, P], U8, align_bytes=64)
+
+        def prepare_rows(pair):
+            for operand, rows in enumerate((x_rows[pair], s_rows[pair])):
+                words = (
+                    rows[:]
+                    .rearrange("p i c -> p (i c)")
+                    .bitcast(F32)
+                    .rearrange("p (i g q u) -> p i g u q", i=PAIR, g=PASSES, u=2)
+                )
+                grouped = stage.tile([P, PAIR * PASSES * P * PACK], BF16, align_bytes=64, tag="a_grouped")
+                grouped_words = grouped[:].bitcast(F32).rearrange(
+                    "p (i g r u) -> p i g r u", i=PAIR, g=PASSES, u=2
+                )
+                for i in range(PAIR):
+                    flipped = psum.tile([P, PASSES * 2, P], F32, tag="bank", name="flipped")
+                    for g in range(PASSES):
+                        for u in range(2):
+                            nc.tensor.transpose(
+                                flipped[:, g * 2 + u, :], words[:, i, g, u, :], identity[:]
+                            )
+                    nc.scalar.copy(
+                        out=grouped_words[:, i],
+                        in_=flipped[:].rearrange("p (g u) r -> p g r u", u=2),
+                    )
+                tiles = slice(pair * PAIR, (pair + 1) * PAIR)
+                nc.vector.quantize_mx(
+                    out=act_codes[:, operand, tiles].rearrange("p i g r -> p (i g r)").bitcast(FP8X4),
+                    scales=act_scales[:, operand, tiles].rearrange("p i g r -> p (i g r)"),
+                    in_=grouped[:],
+                )
+
+        w_grouped = {}
+        w_codes = {}
+        w_scales = {}
+
+        def regroup_weights(index):
+            matrix, g = divmod(index, PASSES)
+            if g == 0:
+                w_grouped[matrix] = stage.tile(
+                    [P, PASSES, HALF, PACK], BF16, align_bytes=64, tag="w_grouped", name="w_grouped"
+                )
+            source = w_raw[index][:].rearrange("p t (c i) -> p c t i", i=4)
+            target = w_grouped[matrix][:, g].rearrange("p (c i) t -> p c t i", i=4)
+            if index < VECTOR_REGROUPS:
+                nc.vector.tensor_copy(out=target, in_=source)
+            else:
+                nc.scalar.copy(out=target, in_=source)
+
+        def quantise_weights(matrix):
+            block, operand = divmod(matrix, OPERANDS)
+            if operand == 0:
+                w_codes[block] = w_mx.tile(
+                    [P, OPERANDS, PASSES, HALF], U32, align_bytes=64, tag="w_codes", name="w_codes"
+                )
+                w_scales[block] = w_mx.tile(
+                    [P, OPERANDS, PASSES, HALF], U8, align_bytes=64, tag="w_scales", name="w_scales"
+                )
+            nc.vector.quantize_mx(
+                out=w_codes[block][:, operand].rearrange("p g c -> p (g c)").bitcast(FP8X4),
+                scales=w_scales[block][:, operand].rearrange("p g c -> p (g c)"),
+                in_=w_grouped[matrix][:].rearrange("p g c t -> p (g c t)"),
+            )
+
+        z_times_s = [
+            keep.tile([P, PAIR, HALF], F32, name="z_times_s%d" % pair) for pair in range(PAIRS)
+        ]
+
+        def gate_values(block, pair):
+            half, gate = divmod(block, GATES)
+            cols = slice(half * HALF, (half + 1) * HALF)
+            biased = work.tile([P, PAIR, HALF], F32, tag="biased")
+            for i in range(PAIR):
+                row_tile = pair * PAIR + i
+                sums = psum.tile([P, HALF], F32, tag="bank", name="sums")
+                for operand in range(OPERANDS):
+                    for g in range(PASSES):
+                        nc.tensor.matmul_mx(
+                            out=sums[:],
+                            lhsT=act_codes[:, operand, row_tile, g, :].bitcast(FP8X4),
+                            lhsT_scale=act_scales[:, operand, row_tile, g, :],
+                            rhs=w_codes[block][:, operand, g, :].bitcast(FP8X4),
+                            rhs_scale=w_scales[block][:, operand, g, :],
+                            start=(operand == 0 and g == 0),
+                            stop=(operand == OPERANDS - 1 and g == PASSES - 1),
+                        )
+                nc.vector.tensor_tensor(
+                    out=biased[:, i, :], in0=sums[:], in1=bias_all[:, gate, cols], op=ALU.add
+                )
+            values = work.tile([P, PAIR, HALF], F32, tag="values", bufs=3)
+            nc.scalar.activation(out=values[:], in_=biased[:], func=TANH)
+            return values
+
+        def mix(block, pair, values):
+            half, gate = divmod(block, GATES)
+            cols = slice(half * HALF, (half + 1) * HALF)
+            if gate == 0:
+                nc.vector.tensor_tensor(
+                    out=z_times_s[pair][:], in0=values[:], in1=s_rows[pair][:, :, cols], op=ALU.mult
+                )
+            else:
+                g_minus_1_times_h = work.tile([P, PAIR, HALF], F32, tag="g_minus_1_times_h")
+                nc.vector.scalar_tensor_tensor(
+                    out=g_minus_1_times_h[:],
+                    in0=values[:],
+                    scalar=1.0,
+                    in1=h_rows[pair][:, :, cols],
+                    op0=ALU.subtract,
+                    op1=ALU.mult,
+                )
+                result = work.tile([P, PAIR, HALF], F32, tag="result")
+                nc.vector.tensor_tensor(
+                    out=result[:], in0=z_times_s[pair][:], in1=g_minus_1_times_h[:], op=ALU.subtract
+                )
+                nc.sync.dma_start(out=row_pair(out, pair)[:, :, cols], in_=result[:])
+
+        prepare_rows(0)
+        for index in range(TILES_PER_BLOCK):
+            regroup_weights(index)
+        for matrix in range(OPERANDS):
+            quantise_weights(matrix)
+
+        unfinished = None
+        for step in range(BLOCKS * PAIRS):
+            block, pair = divmod(step, PAIRS)
+            if pair == 0 and block + 2 < BLOCKS:
+                load_weights(block + 2)
+            if block == 0 and pair + 1 < PAIRS:
+                prepare_rows(pair + 1)
+            index = step + TILES_PER_BLOCK
+            if index < BLOCKS * TILES_PER_BLOCK:
+                regroup_weights(index)
+            values = gate_values(block, pair)
+            if unfinished is not None:
+                mix(*unfinished)
+            if index < BLOCKS * TILES_PER_BLOCK and index % PASSES == PASSES - 1:
+                quantise_weights(index // PASSES)
+            unfinished = (block, pair, values)
+        mix(*unfinished)

@@ -18,15 +18,21 @@ ROWS = 1024
 FEATURES = 1024
 UNITS = 1024
 PASSES = FEATURES // K_PASS
+BANK = 512
 PAIR = 2
+GROUP = BANK // P
 PAIRS = ROWS // (PAIR * P)
-HALF = 512
-HALVES = UNITS // HALF
+GROUPS = ROWS // (GROUP * P)
+HALVES = UNITS // BANK
+UNIT_TILES = BANK // P
 GATES = 2
 OPERANDS = 2
 BLOCKS = HALVES * GATES
 TILES_PER_BLOCK = OPERANDS * PASSES
-VECTOR_REGROUPS = 6
+MATRICES = BLOCKS * OPERANDS
+ROUNDS = HALVES * PAIRS
+UNIT_PAIR = 2
+G_LAG = 2
 
 FLOPS = 2 * ROWS * (OPERANDS * FEATURES) * (GATES * UNITS)
 
@@ -34,14 +40,12 @@ FLOPS = 2 * ROWS * (OPERANDS * FEATURES) * (GATES * UNITS)
 def tile_lstmlayer_pb_kernel(tc, X, S, H, Uz, Ug, Wz, Wg, bz, bg, out):
     nc = tc.nc
     weights = ((Uz, Wz), (Ug, Wg))
-    biases = (bz, bg)
 
     with ExitStack() as ctx:
         const = ctx.enter_context(tc.tile_pool(name="const", bufs=1))
         keep = ctx.enter_context(tc.tile_pool(name="keep", bufs=1))
         w_in = ctx.enter_context(tc.tile_pool(name="w_in", bufs=2 * TILES_PER_BLOCK))
         stage = ctx.enter_context(tc.tile_pool(name="stage", bufs=2))
-        w_mx = ctx.enter_context(tc.tile_pool(name="w_mx", bufs=2))
         work = ctx.enter_context(tc.tile_pool(name="work", bufs=2))
         psum = ctx.enter_context(tc.psum_pool(name="psum", bufs=8))
 
@@ -52,17 +56,21 @@ def tile_lstmlayer_pb_kernel(tc, X, S, H, Uz, Ug, Wz, Wg, bz, bg, out):
         warm = const.tile([P, 1], F32)
         nc.vector.memset(warm[:], 0.0)
         nc.scalar.activation(out=warm[:], in_=warm[:], func=TANH)
-        bias_rows = const.tile([P, GATES, UNITS], BF16)
-        nc.vector.memset(bias_rows[:], 0.0)
+        bz_rows = const.tile([P, UNITS], BF16)
+        nc.vector.memset(bz_rows[:], 0.0)
+        bg_rows = const.tile([P, P], BF16)
+        nc.vector.memset(bg_rows[:], 0.0)
 
-        def row_pair(dram, pair):
-            rows = dram[pair * PAIR * P : (pair + 1) * PAIR * P, :]
+        def row_tiles(dram, first, count):
+            rows = dram[first * P : (first + count) * P, :]
             return rows.rearrange("(i p) c -> p i c", p=P)
 
-        def load_rows(dram, pair, label):
-            loaded = keep.tile([P, PAIR, FEATURES], BF16, name="%s%d" % (label, pair))
-            nc.sync.dma_start(out=loaded[:], in_=row_pair(dram, pair))
-            return loaded
+        def load_pair(loaded, dram, pair):
+            group, second = divmod(pair, GROUP // PAIR)
+            nc.sync.dma_start(
+                out=loaded[group][:, second * PAIR : (second + 1) * PAIR, :],
+                in_=row_tiles(dram, pair * PAIR, PAIR),
+            )
 
         w_raw = {}
 
@@ -70,175 +78,244 @@ def tile_lstmlayer_pb_kernel(tc, X, S, H, Uz, Ug, Wz, Wg, bz, bg, out):
             half, gate = divmod(block, GATES)
             for operand in range(OPERANDS):
                 for g in range(PASSES):
-                    raw = w_in.tile([P, PACK, HALF], BF16, tag="w_raw", name="w_raw")
+                    raw = w_in.tile([P, PACK, BANK], BF16, tag="w_raw", name="w_raw")
                     nc.sync.dma_start(
                         out=raw[:],
                         in_=weights[gate][operand][
-                            g * K_PASS : (g + 1) * K_PASS, half * HALF : (half + 1) * HALF
+                            g * K_PASS : (g + 1) * K_PASS, half * BANK : (half + 1) * BANK
                         ].rearrange("(p t) c -> p t c", t=PACK),
                     )
                     w_raw[(block * OPERANDS + operand) * PASSES + g] = raw
 
-        for gate in range(GATES):
-            nc.sync.dma_start(
-                out=bias_rows[0:1, gate, :], in_=biases[gate].rearrange("(o c) -> o c", o=1)
-            )
-        x_rows = [load_rows(X, 0, "x")]
-        s_rows = [load_rows(S, 0, "s")]
+        x_rows = [keep.tile([P, GROUP, FEATURES], BF16, name="x_rows%d" % n) for n in range(GROUPS)]
+        s_rows = [keep.tile([P, GROUP, UNITS], BF16, name="s_rows%d" % n) for n in range(GROUPS)]
+        h_rows = [keep.tile([P, GROUP, UNITS], BF16, name="h_rows%d" % n) for n in range(GROUPS)]
+
+        nc.sync.dma_start(out=bz_rows[0:1, :], in_=bz.rearrange("(o c) -> o c", o=1))
+        nc.sync.dma_start(out=bg_rows[0 : UNITS // P, :], in_=bg.rearrange("(b u) -> b u", u=P))
+        load_pair(x_rows, X, 0)
+        load_pair(s_rows, S, 0)
         load_weights(0)
-        for pair in range(1, PAIRS):
-            x_rows.append(load_rows(X, pair, "x"))
-            s_rows.append(load_rows(S, pair, "s"))
+        load_pair(x_rows, X, 1)
+        load_pair(s_rows, S, 1)
         load_weights(1)
-        h_rows = [load_rows(H, pair, "h") for pair in range(PAIRS)]
+        for pair in range(GROUP // PAIR, PAIRS):
+            load_pair(x_rows, X, pair)
+            load_pair(s_rows, S, pair)
+            load_pair(h_rows, H, 2 * (pair - GROUP // PAIR))
+            load_pair(h_rows, H, 2 * (pair - GROUP // PAIR) + 1)
 
-        bias_all = const.tile([P, GATES, UNITS], F32)
-        for gate in range(GATES):
-            for half in range(HALVES):
-                cols = slice(half * HALF, (half + 1) * HALF)
-                spread = psum.tile([P, HALF], F32, tag="bank", name="spread")
-                nc.tensor.matmul(
-                    out=spread[:], lhsT=ones[:], rhs=bias_rows[:, gate, cols], start=True, stop=True
-                )
-                nc.scalar.copy(out=bias_all[:, gate, cols], in_=spread[:])
+        bz_all = const.tile([P, UNITS], F32)
+        for half in range(HALVES):
+            cols = slice(half * BANK, (half + 1) * BANK)
+            spread = psum.tile([P, BANK], F32, tag="bank", name="spread")
+            nc.tensor.matmul(out=spread[:], lhsT=ones[:], rhs=bz_rows[:, cols], start=True, stop=True)
+            nc.scalar.copy(out=bz_all[:, cols], in_=spread[:])
+        bg_wide = const.tile([P, P], F32)
+        nc.vector.tensor_copy(out=bg_wide[:], in_=bg_rows[:])
+        bg_flipped = psum.tile([P, P], F32, tag="bank", name="bg_flipped")
+        nc.tensor.transpose(bg_flipped[:], bg_wide[:], identity[:])
+        bg_columns = const.tile([P, UNITS // P], F32)
+        nc.scalar.copy(out=bg_columns[:], in_=bg_flipped[:, 0 : UNITS // P])
 
-        act_codes = keep.tile([P, OPERANDS, PAIRS * PAIR, PASSES, P], U32, align_bytes=64)
-        act_scales = keep.tile([P, OPERANDS, PAIRS * PAIR, PASSES, P], U8, align_bytes=64)
+        act_codes = keep.tile([P, OPERANDS, PASSES, ROWS], U32, align_bytes=64)
+        act_scales = keep.tile([P, OPERANDS, PASSES, ROWS], U8, align_bytes=64)
 
         def prepare_rows(pair):
-            for operand, rows in enumerate((x_rows[pair], s_rows[pair])):
+            group, second = divmod(pair, GROUP // PAIR)
+            for operand, loaded in enumerate((x_rows[group], s_rows[group])):
                 words = (
-                    rows[:]
+                    loaded[:]
                     .rearrange("p i c -> p (i c)")
                     .bitcast(F32)
-                    .rearrange("p (i g q u) -> p i g u q", i=PAIR, g=PASSES, u=2)
+                    .rearrange("p (i g q u) -> p i g u q", i=GROUP, g=PASSES, u=2)
                 )
-                grouped = stage.tile([P, PAIR * PASSES * P * PACK], BF16, align_bytes=64, tag="a_grouped")
-                grouped_words = grouped[:].bitcast(F32).rearrange(
-                    "p (i g r u) -> p i g r u", i=PAIR, g=PASSES, u=2
+                grouped = stage.tile([P, PASSES, PAIR * P * PACK], BF16, align_bytes=64, tag="a_grouped")
+                grouped_words = (
+                    grouped[:]
+                    .rearrange("p g c -> p (g c)")
+                    .bitcast(F32)
+                    .rearrange("p (g i r u) -> p i g r u", g=PASSES, i=PAIR, u=2)
                 )
                 for i in range(PAIR):
                     flipped = psum.tile([P, PASSES * 2, P], F32, tag="bank", name="flipped")
                     for g in range(PASSES):
                         for u in range(2):
                             nc.tensor.transpose(
-                                flipped[:, g * 2 + u, :], words[:, i, g, u, :], identity[:]
+                                flipped[:, g * 2 + u, :],
+                                words[:, second * PAIR + i, g, u, :],
+                                identity[:],
                             )
                     nc.scalar.copy(
                         out=grouped_words[:, i],
                         in_=flipped[:].rearrange("p (g u) r -> p g r u", u=2),
                     )
-                tiles = slice(pair * PAIR, (pair + 1) * PAIR)
-                nc.vector.quantize_mx(
-                    out=act_codes[:, operand, tiles].rearrange("p i g r -> p (i g r)").bitcast(FP8X4),
-                    scales=act_scales[:, operand, tiles].rearrange("p i g r -> p (i g r)"),
-                    in_=grouped[:],
-                )
+                rows = slice(pair * PAIR * P, (pair + 1) * PAIR * P)
+                for g in range(PASSES):
+                    nc.vector.quantize_mx(
+                        out=act_codes[:, operand, g, rows].bitcast(FP8X4),
+                        scales=act_scales[:, operand, g, rows],
+                        in_=grouped[:, g, :],
+                    )
 
+        w_codes = [
+            keep.tile([P, OPERANDS, PASSES, BANK], U32, align_bytes=64, name="w_codes%d" % n)
+            for n in range(BLOCKS)
+        ]
+        w_scales = [
+            keep.tile([P, OPERANDS, PASSES, BANK], U8, align_bytes=64, name="w_scales%d" % n)
+            for n in range(BLOCKS)
+        ]
         w_grouped = {}
-        w_codes = {}
-        w_scales = {}
 
-        def regroup_weights(index):
-            matrix, g = divmod(index, PASSES)
-            if g == 0:
-                w_grouped[matrix] = stage.tile(
-                    [P, PASSES, HALF, PACK], BF16, align_bytes=64, tag="w_grouped", name="w_grouped"
+        def regroup_weights(matrix):
+            grouped = stage.tile([P, PASSES, BANK, PACK], BF16, align_bytes=64, tag="w_grouped")
+            for g, copy in enumerate((nc.vector.tensor_copy, nc.scalar.copy)):
+                copy(
+                    out=grouped[:, g].rearrange("p (c i) t -> p c t i", i=4),
+                    in_=w_raw[matrix * PASSES + g][:].rearrange("p t (c i) -> p c t i", i=4),
                 )
-            source = w_raw[index][:].rearrange("p t (c i) -> p c t i", i=4)
-            target = w_grouped[matrix][:, g].rearrange("p (c i) t -> p c t i", i=4)
-            if index < VECTOR_REGROUPS:
-                nc.vector.tensor_copy(out=target, in_=source)
-            else:
-                nc.scalar.copy(out=target, in_=source)
+            w_grouped[matrix] = grouped
 
         def quantise_weights(matrix):
             block, operand = divmod(matrix, OPERANDS)
-            if operand == 0:
-                w_codes[block] = w_mx.tile(
-                    [P, OPERANDS, PASSES, HALF], U32, align_bytes=64, tag="w_codes", name="w_codes"
-                )
-                w_scales[block] = w_mx.tile(
-                    [P, OPERANDS, PASSES, HALF], U8, align_bytes=64, tag="w_scales", name="w_scales"
-                )
             nc.vector.quantize_mx(
                 out=w_codes[block][:, operand].rearrange("p g c -> p (g c)").bitcast(FP8X4),
                 scales=w_scales[block][:, operand].rearrange("p g c -> p (g c)"),
                 in_=w_grouped[matrix][:].rearrange("p g c t -> p (g c t)"),
             )
 
-        z_times_s = [
-            keep.tile([P, PAIR, HALF], F32, name="z_times_s%d" % pair) for pair in range(PAIRS)
-        ]
+        z_values = {}
+        z_times_s = {}
 
-        def gate_values(block, pair):
-            half, gate = divmod(block, GATES)
-            cols = slice(half * HALF, (half + 1) * HALF)
-            biased = work.tile([P, PAIR, HALF], F32, tag="biased")
+        def z_sums(z_round):
+            half, pair = divmod(z_round, PAIRS)
+            block = half * GATES
+            biased = work.tile([P, PAIR, BANK], F32, tag="biased")
             for i in range(PAIR):
-                row_tile = pair * PAIR + i
-                sums = psum.tile([P, HALF], F32, tag="bank", name="sums")
+                rows = slice((pair * PAIR + i) * P, (pair * PAIR + i + 1) * P)
+                sums = psum.tile([P, BANK], F32, tag="bank", name="sums")
                 for operand in range(OPERANDS):
                     for g in range(PASSES):
                         nc.tensor.matmul_mx(
                             out=sums[:],
-                            lhsT=act_codes[:, operand, row_tile, g, :].bitcast(FP8X4),
-                            lhsT_scale=act_scales[:, operand, row_tile, g, :],
+                            lhsT=act_codes[:, operand, g, rows].bitcast(FP8X4),
+                            lhsT_scale=act_scales[:, operand, g, rows],
                             rhs=w_codes[block][:, operand, g, :].bitcast(FP8X4),
                             rhs_scale=w_scales[block][:, operand, g, :],
                             start=(operand == 0 and g == 0),
                             stop=(operand == OPERANDS - 1 and g == PASSES - 1),
                         )
                 nc.vector.tensor_tensor(
-                    out=biased[:, i, :], in0=sums[:], in1=bias_all[:, gate, cols], op=ALU.add
+                    out=biased[:, i, :],
+                    in0=sums[:],
+                    in1=bz_all[:, half * BANK : (half + 1) * BANK],
+                    op=ALU.add,
                 )
-            values = work.tile([P, PAIR, HALF], F32, tag="values", bufs=3)
-            nc.scalar.activation(out=values[:], in_=biased[:], func=TANH)
-            return values
+            z = work.tile([P, PAIR, BANK], F32, tag="z", bufs=3)
+            nc.scalar.activation(out=z[:], in_=biased[:], func=TANH)
+            z_values[z_round] = z
 
-        def mix(block, pair, values):
-            half, gate = divmod(block, GATES)
-            cols = slice(half * HALF, (half + 1) * HALF)
-            if gate == 0:
-                nc.vector.tensor_tensor(
-                    out=z_times_s[pair][:], in0=values[:], in1=s_rows[pair][:, :, cols], op=ALU.mult
+        def z_product(z_round):
+            half, pair = divmod(z_round, PAIRS)
+            group, second = divmod(pair, GROUP // PAIR)
+            if second == 0:
+                z_times_s[(half, group)] = work.tile([P, GROUP, BANK], F32, tag="z_times_s", name="z_times_s")
+            tiles = slice(second * PAIR, (second + 1) * PAIR)
+            nc.vector.tensor_tensor(
+                out=z_times_s[(half, group)][:, tiles, :],
+                in0=z_values[z_round][:],
+                in1=s_rows[group][:, tiles, half * BANK : (half + 1) * BANK],
+                op=ALU.mult,
+            )
+
+        g_by_unit = {}
+
+        def g_sums(g_round):
+            step, unit_pair = divmod(g_round, UNIT_TILES // UNIT_PAIR)
+            half, group = divmod(step, GROUPS)
+            block = half * GATES + 1
+            rows = slice(group * GROUP * P, (group + 1) * GROUP * P)
+            for j in range(UNIT_PAIR):
+                unit_tile = unit_pair * UNIT_PAIR + j
+                units = slice(unit_tile * P, (unit_tile + 1) * P)
+                sums = psum.tile([P, BANK], F32, tag="bank", name="sums_by_unit")
+                for operand in range(OPERANDS):
+                    for g in range(PASSES):
+                        nc.tensor.matmul_mx(
+                            out=sums[:],
+                            lhsT=w_codes[block][:, operand, g, units].bitcast(FP8X4),
+                            lhsT_scale=w_scales[block][:, operand, g, units],
+                            rhs=act_codes[:, operand, g, rows].bitcast(FP8X4),
+                            rhs_scale=act_scales[:, operand, g, rows],
+                            start=(operand == 0 and g == 0),
+                            stop=(operand == OPERANDS - 1 and g == PASSES - 1),
+                        )
+                column = half * UNIT_TILES + unit_tile
+                values = work.tile([P, GROUP, P], F32, tag="g_by_unit", bufs=2 * UNIT_PAIR)
+                nc.scalar.activation(
+                    out=values[:].rearrange("p i r -> p (i r)"),
+                    in_=sums[:],
+                    func=TANH,
+                    bias=bg_columns[:, column : column + 1],
                 )
-            else:
-                g_minus_1_times_h = work.tile([P, PAIR, HALF], F32, tag="g_minus_1_times_h")
+                g_by_unit[(g_round, j)] = values
+
+        def g_finish(g_round):
+            step, unit_pair = divmod(g_round, UNIT_TILES // UNIT_PAIR)
+            half, group = divmod(step, GROUPS)
+            flipped = []
+            for j in range(UNIT_PAIR):
+                g_by_row = psum.tile([P, GROUP, P], F32, tag="bank", name="g_by_row")
+                for i in range(GROUP):
+                    nc.tensor.transpose(g_by_row[:, i, :], g_by_unit[(g_round, j)][:, i, :], identity[:])
+                flipped.append(g_by_row)
+            result = work.tile([P, GROUP, UNIT_PAIR * P], F32, tag="result", bufs=3)
+            first = unit_pair * UNIT_PAIR * P
+            for j in range(UNIT_PAIR):
+                units = slice(half * BANK + first + j * P, half * BANK + first + (j + 1) * P)
                 nc.vector.scalar_tensor_tensor(
-                    out=g_minus_1_times_h[:],
-                    in0=values[:],
+                    out=result[:, :, j * P : (j + 1) * P],
+                    in0=flipped[j][:],
                     scalar=1.0,
-                    in1=h_rows[pair][:, :, cols],
+                    in1=h_rows[group][:, :, units],
                     op0=ALU.subtract,
                     op1=ALU.mult,
                 )
-                result = work.tile([P, PAIR, HALF], F32, tag="result")
-                nc.vector.tensor_tensor(
-                    out=result[:], in0=z_times_s[pair][:], in1=g_minus_1_times_h[:], op=ALU.subtract
-                )
-                nc.sync.dma_start(out=row_pair(out, pair)[:, :, cols], in_=result[:])
+            nc.vector.tensor_tensor(
+                out=result[:],
+                in0=z_times_s[(half, group)][:, :, first : first + UNIT_PAIR * P],
+                in1=result[:],
+                op=ALU.subtract,
+            )
+            nc.sync.dma_start(
+                out=row_tiles(out, group * GROUP, GROUP)[
+                    :, :, half * BANK + first : half * BANK + first + UNIT_PAIR * P
+                ],
+                in_=result[:],
+            )
 
         prepare_rows(0)
-        for index in range(TILES_PER_BLOCK):
-            regroup_weights(index)
+        for matrix in range(OPERANDS):
+            regroup_weights(matrix)
         for matrix in range(OPERANDS):
             quantise_weights(matrix)
 
-        unfinished = None
-        for step in range(BLOCKS * PAIRS):
-            block, pair = divmod(step, PAIRS)
-            if pair == 0 and block + 2 < BLOCKS:
-                load_weights(block + 2)
-            if block == 0 and pair + 1 < PAIRS:
-                prepare_rows(pair + 1)
-            index = step + TILES_PER_BLOCK
-            if index < BLOCKS * TILES_PER_BLOCK:
-                regroup_weights(index)
-            values = gate_values(block, pair)
-            if unfinished is not None:
-                mix(*unfinished)
-            if index < BLOCKS * TILES_PER_BLOCK and index % PASSES == PASSES - 1:
-                quantise_weights(index // PASSES)
-            unfinished = (block, pair, values)
-        mix(*unfinished)
+        for n in range(ROUNDS + G_LAG + 1):
+            if n + 1 < PAIRS:
+                prepare_rows(n + 1)
+            matrix = n + OPERANDS
+            if matrix < MATRICES:
+                regroup_weights(matrix)
+                if matrix % OPERANDS == 0 and matrix // OPERANDS + 1 < BLOCKS:
+                    load_weights(matrix // OPERANDS + 1)
+            if n < ROUNDS:
+                z_sums(n)
+            if 0 <= n - G_LAG < ROUNDS:
+                g_sums(n - G_LAG)
+            if 0 <= n - 1 < ROUNDS:
+                z_product(n - 1)
+            if 0 <= n - G_LAG - 1 < ROUNDS:
+                g_finish(n - G_LAG - 1)
+            if matrix < MATRICES:
+                quantise_weights(matrix)

@@ -61,16 +61,14 @@ def tile_lstmlayer_pb_kernel(tc, X, S, H, Uz, Ug, Wz, Wg, bz, bg, out):
         bg_rows = const.tile([P, P], BF16)
         nc.vector.memset(bg_rows[:], 0.0)
 
-        def row_tiles(dram, first, count):
-            rows = dram[first * P : (first + count) * P, :]
-            return rows.rearrange("(i p) c -> p i c", p=P)
+        def group_rows(dram, group):
+            rows = dram[group * GROUP * P : (group + 1) * GROUP * P, :]
+            return rows.rearrange("(p i) c -> p i c", i=GROUP)
 
         def load_pair(loaded, dram, pair):
             group, second = divmod(pair, GROUP // PAIR)
-            nc.sync.dma_start(
-                out=loaded[group][:, second * PAIR : (second + 1) * PAIR, :],
-                in_=row_tiles(dram, pair * PAIR, PAIR),
-            )
+            tiles = slice(second * PAIR, (second + 1) * PAIR)
+            nc.sync.dma_start(out=loaded[group][:, tiles, :], in_=group_rows(dram, group)[:, tiles, :])
 
         w_raw = {}
 
@@ -99,11 +97,12 @@ def tile_lstmlayer_pb_kernel(tc, X, S, H, Uz, Ug, Wz, Wg, bz, bg, out):
         load_pair(x_rows, X, 1)
         load_pair(s_rows, S, 1)
         load_weights(1)
-        for pair in range(GROUP // PAIR, PAIRS):
-            load_pair(x_rows, X, pair)
-            load_pair(s_rows, S, pair)
-            load_pair(h_rows, H, 2 * (pair - GROUP // PAIR))
-            load_pair(h_rows, H, 2 * (pair - GROUP // PAIR) + 1)
+        load_pair(x_rows, X, 2)
+        load_pair(s_rows, S, 2)
+        load_pair(h_rows, H, 0)
+        load_pair(h_rows, H, 1)
+        load_pair(x_rows, X, 3)
+        load_pair(s_rows, S, 3)
 
         bz_all = const.tile([P, UNITS], F32)
         for half in range(HALVES):
@@ -176,6 +175,9 @@ def tile_lstmlayer_pb_kernel(tc, X, S, H, Uz, Ug, Wz, Wg, bz, bg, out):
                     in_=w_raw[matrix * PASSES + g][:].rearrange("p t (c i) -> p c t i", i=4),
                 )
             w_grouped[matrix] = grouped
+            block, operand = divmod(matrix, OPERANDS)
+            if operand == OPERANDS - 1 and block + 2 < BLOCKS:
+                load_weights(block + 2)
 
         def quantise_weights(matrix):
             block, operand = divmod(matrix, OPERANDS)
@@ -289,7 +291,7 @@ def tile_lstmlayer_pb_kernel(tc, X, S, H, Uz, Ug, Wz, Wg, bz, bg, out):
                 op=ALU.subtract,
             )
             nc.sync.dma_start(
-                out=row_tiles(out, group * GROUP, GROUP)[
+                out=group_rows(out, group)[
                     :, :, half * BANK + first : half * BANK + first + UNIT_PAIR * P
                 ],
                 in_=result[:],
@@ -298,6 +300,8 @@ def tile_lstmlayer_pb_kernel(tc, X, S, H, Uz, Ug, Wz, Wg, bz, bg, out):
         prepare_rows(0)
         for matrix in range(OPERANDS):
             regroup_weights(matrix)
+        load_pair(h_rows, H, 2)
+        load_pair(h_rows, H, 3)
         for matrix in range(OPERANDS):
             quantise_weights(matrix)
 
@@ -307,8 +311,6 @@ def tile_lstmlayer_pb_kernel(tc, X, S, H, Uz, Ug, Wz, Wg, bz, bg, out):
             matrix = n + OPERANDS
             if matrix < MATRICES:
                 regroup_weights(matrix)
-                if matrix % OPERANDS == 0 and matrix // OPERANDS + 1 < BLOCKS:
-                    load_weights(matrix // OPERANDS + 1)
             if n < ROUNDS:
                 z_sums(n)
             if 0 <= n - G_LAG < ROUNDS:

@@ -32,6 +32,7 @@ TILES_PER_BLOCK = OPERANDS * PASSES
 MATRICES = BLOCKS * OPERANDS
 ROUNDS = HALVES * PAIRS
 UNIT_PAIR = 2
+SCALAR_ALONE_FROM = 6
 G_LAG = 2
 
 FLOPS = 2 * ROWS * (OPERANDS * FEATURES) * (GATES * UNITS)
@@ -99,10 +100,10 @@ def tile_lstmlayer_pb_kernel(tc, X, S, H, Uz, Ug, Wz, Wg, bz, bg, out):
         load_weights(1)
         load_pair(x_rows, X, 2)
         load_pair(s_rows, S, 2)
-        load_pair(h_rows, H, 0)
-        load_pair(h_rows, H, 1)
         load_pair(x_rows, X, 3)
         load_pair(s_rows, S, 3)
+        load_pair(h_rows, H, 0)
+        load_pair(h_rows, H, 1)
 
         bz_all = const.tile([P, UNITS], F32)
         for half in range(HALVES):
@@ -169,7 +170,8 @@ def tile_lstmlayer_pb_kernel(tc, X, S, H, Uz, Ug, Wz, Wg, bz, bg, out):
 
         def regroup_weights(matrix):
             grouped = stage.tile([P, PASSES, BANK, PACK], BF16, align_bytes=64, tag="w_grouped")
-            for g, copy in enumerate((nc.vector.tensor_copy, nc.scalar.copy)):
+            first_copy = nc.scalar.copy if matrix >= SCALAR_ALONE_FROM else nc.vector.tensor_copy
+            for g, copy in enumerate((first_copy, nc.scalar.copy)):
                 copy(
                     out=grouped[:, g].rearrange("p (c i) t -> p c t i", i=4),
                     in_=w_raw[matrix * PASSES + g][:].rearrange("p t (c i) -> p c t i", i=4),
@@ -233,12 +235,12 @@ def tile_lstmlayer_pb_kernel(tc, X, S, H, Uz, Ug, Wz, Wg, bz, bg, out):
 
         g_by_unit = {}
 
-        def g_sums(g_round):
+        def g_sums(g_round, tiles=(0, 1)):
             step, unit_pair = divmod(g_round, UNIT_TILES // UNIT_PAIR)
             half, group = divmod(step, GROUPS)
             block = half * GATES + 1
             rows = slice(group * GROUP * P, (group + 1) * GROUP * P)
-            for j in range(UNIT_PAIR):
+            for j in tiles:
                 unit_tile = unit_pair * UNIT_PAIR + j
                 units = slice(unit_tile * P, (unit_tile + 1) * P)
                 sums = psum.tile([P, BANK], F32, tag="bank", name="sums_by_unit")
@@ -263,21 +265,22 @@ def tile_lstmlayer_pb_kernel(tc, X, S, H, Uz, Ug, Wz, Wg, bz, bg, out):
                 )
                 g_by_unit[(g_round, j)] = values
 
-        def g_finish(g_round):
+        def g_finish(g_round, tiles=(0, 1)):
             step, unit_pair = divmod(g_round, UNIT_TILES // UNIT_PAIR)
             half, group = divmod(step, GROUPS)
-            flipped = []
-            for j in range(UNIT_PAIR):
+            flipped = {}
+            for j in tiles:
                 g_by_row = psum.tile([P, GROUP, P], F32, tag="bank", name="g_by_row")
                 for i in range(GROUP):
                     nc.tensor.transpose(g_by_row[:, i, :], g_by_unit[(g_round, j)][:, i, :], identity[:])
-                flipped.append(g_by_row)
+                flipped[j] = g_by_row
+            width = len(tiles) * P
             result = work.tile([P, GROUP, UNIT_PAIR * P], F32, tag="result", bufs=3)
-            first = unit_pair * UNIT_PAIR * P
-            for j in range(UNIT_PAIR):
-                units = slice(half * BANK + first + j * P, half * BANK + first + (j + 1) * P)
+            first = (unit_pair * UNIT_PAIR + tiles[0]) * P
+            for n_th, j in enumerate(tiles):
+                units = slice(half * BANK + first + n_th * P, half * BANK + first + (n_th + 1) * P)
                 nc.vector.scalar_tensor_tensor(
-                    out=result[:, :, j * P : (j + 1) * P],
+                    out=result[:, :, n_th * P : (n_th + 1) * P],
                     in0=flipped[j][:],
                     scalar=1.0,
                     in1=h_rows[group][:, :, units],
@@ -285,16 +288,14 @@ def tile_lstmlayer_pb_kernel(tc, X, S, H, Uz, Ug, Wz, Wg, bz, bg, out):
                     op1=ALU.mult,
                 )
             nc.vector.tensor_tensor(
-                out=result[:],
-                in0=z_times_s[(half, group)][:, :, first : first + UNIT_PAIR * P],
-                in1=result[:],
+                out=result[:, :, 0:width],
+                in0=z_times_s[(half, group)][:, :, first : first + width],
+                in1=result[:, :, 0:width],
                 op=ALU.subtract,
             )
             nc.sync.dma_start(
-                out=group_rows(out, group)[
-                    :, :, half * BANK + first : half * BANK + first + UNIT_PAIR * P
-                ],
-                in_=result[:],
+                out=group_rows(out, group)[:, :, half * BANK + first : half * BANK + first + width],
+                in_=result[:, :, 0:width],
             )
 
         prepare_rows(0)
@@ -313,6 +314,13 @@ def tile_lstmlayer_pb_kernel(tc, X, S, H, Uz, Ug, Wz, Wg, bz, bg, out):
                 regroup_weights(matrix)
             if n < ROUNDS:
                 z_sums(n)
+            if n - G_LAG == ROUNDS - 1:
+                g_sums(ROUNDS - 1, (0,))
+                g_finish(ROUNDS - 2)
+                g_sums(ROUNDS - 1, (1,))
+                g_finish(ROUNDS - 1, (0,))
+                g_finish(ROUNDS - 1, (1,))
+                break
             if 0 <= n - G_LAG < ROUNDS:
                 g_sums(n - G_LAG)
             if 0 <= n - 1 < ROUNDS:

from contextlib import ExitStack

import concourse.mybir as mybir
from concourse.masks import make_identity

F32 = mybir.dt.float32
BF16 = mybir.dt.bfloat16
U32 = mybir.dt.uint32
U8 = mybir.dt.uint8
FP8X4 = mybir.dt.float8_e4m3fn_x4
ALU = mybir.AluOpType
TANH = mybir.ActivationFunctionType.Tanh

P = 128
PACK = 4
K_PASS = P * PACK
ROWS = 1024
FEATURES = 1024
UNITS = 1024
PASSES = FEATURES // K_PASS
BANK = 512
PAIR = 2
GROUP = BANK // P
PAIRS = ROWS // (PAIR * P)
GROUPS = ROWS // (GROUP * P)
HALVES = UNITS // BANK
UNIT_TILES = BANK // P
GATES = 2
OPERANDS = 2
BLOCKS = HALVES * GATES
TILES_PER_BLOCK = OPERANDS * PASSES
MATRICES = BLOCKS * OPERANDS
ROUNDS = HALVES * PAIRS
UNIT_PAIR = 2
SCALAR_ALONE_FROM = 6
G_LAG = 2

FLOPS = 2 * ROWS * (OPERANDS * FEATURES) * (GATES * UNITS)


def tile_lstmlayer_pb_kernel(tc, X, S, H, Uz, Ug, Wz, Wg, bz, bg, out):
    nc = tc.nc
    weights = ((Uz, Wz), (Ug, Wg))

    with ExitStack() as ctx:
        const = ctx.enter_context(tc.tile_pool(name="const", bufs=1))
        keep = ctx.enter_context(tc.tile_pool(name="keep", bufs=1))
        w_in = ctx.enter_context(tc.tile_pool(name="w_in", bufs=2 * TILES_PER_BLOCK))
        stage = ctx.enter_context(tc.tile_pool(name="stage", bufs=2))
        work = ctx.enter_context(tc.tile_pool(name="work", bufs=2))
        psum = ctx.enter_context(tc.psum_pool(name="psum", bufs=8))

        identity = const.tile([P, P], F32)
        make_identity(nc, identity[:])
        ones = const.tile([P, P], BF16)
        nc.vector.memset(ones[:], 1.0)
        warm = const.tile([P, 1], F32)
        nc.vector.memset(warm[:], 0.0)
        nc.scalar.activation(out=warm[:], in_=warm[:], func=TANH)
        bz_rows = const.tile([P, UNITS], BF16)
        nc.vector.memset(bz_rows[:], 0.0)
        bg_rows = const.tile([P, P], BF16)
        nc.vector.memset(bg_rows[:], 0.0)

        def group_rows(dram, group):
            rows = dram[group * GROUP * P : (group + 1) * GROUP * P, :]
            return rows.rearrange("(p i) c -> p i c", i=GROUP)

        def load_pair(loaded, dram, pair):
            group, second = divmod(pair, GROUP // PAIR)
            tiles = slice(second * PAIR, (second + 1) * PAIR)
            nc.sync.dma_start(out=loaded[group][:, tiles, :], in_=group_rows(dram, group)[:, tiles, :])

        w_raw = {}

        def load_weights(block):
            half, gate = divmod(block, GATES)
            for operand in range(OPERANDS):
                for g in range(PASSES):
                    raw = w_in.tile([P, PACK, BANK], BF16, tag="w_raw", name="w_raw")
                    nc.sync.dma_start(
                        out=raw[:],
                        in_=weights[gate][operand][
                            g * K_PASS : (g + 1) * K_PASS, half * BANK : (half + 1) * BANK
                        ].rearrange("(p t) c -> p t c", t=PACK),
                    )
                    w_raw[(block * OPERANDS + operand) * PASSES + g] = raw

        x_rows = [keep.tile([P, GROUP, FEATURES], BF16, name="x_rows%d" % n) for n in range(GROUPS)]
        s_rows = [keep.tile([P, GROUP, UNITS], BF16, name="s_rows%d" % n) for n in range(GROUPS)]
        h_rows = [keep.tile([P, GROUP, UNITS], BF16, name="h_rows%d" % n) for n in range(GROUPS)]

        nc.sync.dma_start(out=bz_rows[0:1, :], in_=bz.rearrange("(o c) -> o c", o=1))
        nc.sync.dma_start(out=bg_rows[0 : UNITS // P, :], in_=bg.rearrange("(b u) -> b u", u=P))
        load_pair(x_rows, X, 0)
        load_pair(s_rows, S, 0)
        load_weights(0)
        load_pair(x_rows, X, 1)
        load_pair(s_rows, S, 1)
        load_weights(1)
        load_pair(x_rows, X, 2)
        load_pair(s_rows, S, 2)
        load_pair(x_rows, X, 3)
        load_pair(s_rows, S, 3)
        load_pair(h_rows, H, 0)
        load_pair(h_rows, H, 1)

        bz_all = const.tile([P, UNITS], F32)
        for half in range(HALVES):
            cols = slice(half * BANK, (half + 1) * BANK)
            spread = psum.tile([P, BANK], F32, tag="bank", name="spread")
            nc.tensor.matmul(out=spread[:], lhsT=ones[:], rhs=bz_rows[:, cols], start=True, stop=True)
            nc.scalar.copy(out=bz_all[:, cols], in_=spread[:])
        bg_wide = const.tile([P, P], F32)
        nc.vector.tensor_copy(out=bg_wide[:], in_=bg_rows[:])
        bg_flipped = psum.tile([P, P], F32, tag="bank", name="bg_flipped")
        nc.tensor.transpose(bg_flipped[:], bg_wide[:], identity[:])
        bg_columns = const.tile([P, UNITS // P], F32)
        nc.scalar.copy(out=bg_columns[:], in_=bg_flipped[:, 0 : UNITS // P])

        act_codes = keep.tile([P, OPERANDS, PASSES, ROWS], U32, align_bytes=64)
        act_scales = keep.tile([P, OPERANDS, PASSES, ROWS], U8, align_bytes=64)

        def prepare_rows(pair):
            group, second = divmod(pair, GROUP // PAIR)
            for operand, loaded in enumerate((x_rows[group], s_rows[group])):
                words = (
                    loaded[:]
                    .rearrange("p i c -> p (i c)")
                    .bitcast(F32)
                    .rearrange("p (i g q u) -> p i g u q", i=GROUP, g=PASSES, u=2)
                )
                grouped = stage.tile([P, PASSES, PAIR * P * PACK], BF16, align_bytes=64, tag="a_grouped")
                grouped_words = (
                    grouped[:]
                    .rearrange("p g c -> p (g c)")
                    .bitcast(F32)
                    .rearrange("p (g i r u) -> p i g r u", g=PASSES, i=PAIR, u=2)
                )
                for i in range(PAIR):
                    flipped = psum.tile([P, PASSES * 2, P], F32, tag="bank", name="flipped")
                    for g in range(PASSES):
                        for u in range(2):
                            nc.tensor.transpose(
                                flipped[:, g * 2 + u, :],
                                words[:, second * PAIR + i, g, u, :],
                                identity[:],
                            )
                    nc.scalar.copy(
                        out=grouped_words[:, i],
                        in_=flipped[:].rearrange("p (g u) r -> p g r u", u=2),
                    )
                rows = slice(pair * PAIR * P, (pair + 1) * PAIR * P)
                for g in range(PASSES):
                    nc.vector.quantize_mx(
                        out=act_codes[:, operand, g, rows].bitcast(FP8X4),
                        scales=act_scales[:, operand, g, rows],
                        in_=grouped[:, g, :],
                    )

        w_codes = [
            keep.tile([P, OPERANDS, PASSES, BANK], U32, align_bytes=64, name="w_codes%d" % n)
            for n in range(BLOCKS)
        ]
        w_scales = [
            keep.tile([P, OPERANDS, PASSES, BANK], U8, align_bytes=64, name="w_scales%d" % n)
            for n in range(BLOCKS)
        ]
        w_grouped = {}

        def regroup_weights(matrix):
            grouped = stage.tile([P, PASSES, BANK, PACK], BF16, align_bytes=64, tag="w_grouped")
            first_copy = nc.scalar.copy if matrix >= SCALAR_ALONE_FROM else nc.vector.tensor_copy
            for g, copy in enumerate((first_copy, nc.scalar.copy)):
                copy(
                    out=grouped[:, g].rearrange("p (c i) t -> p c t i", i=4),
                    in_=w_raw[matrix * PASSES + g][:].rearrange("p t (c i) -> p c t i", i=4),
                )
            w_grouped[matrix] = grouped
            block, operand = divmod(matrix, OPERANDS)
            if operand == OPERANDS - 1 and block + 2 < BLOCKS:
                load_weights(block + 2)

        def quantise_weights(matrix):
            block, operand = divmod(matrix, OPERANDS)
            nc.vector.quantize_mx(
                out=w_codes[block][:, operand].rearrange("p g c -> p (g c)").bitcast(FP8X4),
                scales=w_scales[block][:, operand].rearrange("p g c -> p (g c)"),
                in_=w_grouped[matrix][:].rearrange("p g c t -> p (g c t)"),
            )

        z_values = {}
        z_times_s = {}

        def z_sums(z_round):
            half, pair = divmod(z_round, PAIRS)
            block = half * GATES
            biased = work.tile([P, PAIR, BANK], F32, tag="biased")
            for i in range(PAIR):
                rows = slice((pair * PAIR + i) * P, (pair * PAIR + i + 1) * P)
                sums = psum.tile([P, BANK], F32, tag="bank", name="sums")
                for operand in range(OPERANDS):
                    for g in range(PASSES):
                        nc.tensor.matmul_mx(
                            out=sums[:],
                            lhsT=act_codes[:, operand, g, rows].bitcast(FP8X4),
                            lhsT_scale=act_scales[:, operand, g, rows],
                            rhs=w_codes[block][:, operand, g, :].bitcast(FP8X4),
                            rhs_scale=w_scales[block][:, operand, g, :],
                            start=(operand == 0 and g == 0),
                            stop=(operand == OPERANDS - 1 and g == PASSES - 1),
                        )
                nc.vector.tensor_tensor(
                    out=biased[:, i, :],
                    in0=sums[:],
                    in1=bz_all[:, half * BANK : (half + 1) * BANK],
                    op=ALU.add,
                )
            z = work.tile([P, PAIR, BANK], F32, tag="z", bufs=3)
            nc.scalar.activation(out=z[:], in_=biased[:], func=TANH)
            z_values[z_round] = z

        def z_product(z_round):
            half, pair = divmod(z_round, PAIRS)
            group, second = divmod(pair, GROUP // PAIR)
            if second == 0:
                z_times_s[(half, group)] = work.tile([P, GROUP, BANK], F32, tag="z_times_s", name="z_times_s")
            tiles = slice(second * PAIR, (second + 1) * PAIR)
            nc.vector.tensor_tensor(
                out=z_times_s[(half, group)][:, tiles, :],
                in0=z_values[z_round][:],
                in1=s_rows[group][:, tiles, half * BANK : (half + 1) * BANK],
                op=ALU.mult,
            )

        g_by_unit = {}

        def g_sums(g_round, tiles=(0, 1)):
            step, unit_pair = divmod(g_round, UNIT_TILES // UNIT_PAIR)
            half, group = divmod(step, GROUPS)
            block = half * GATES + 1
            rows = slice(group * GROUP * P, (group + 1) * GROUP * P)
            for j in tiles:
                unit_tile = unit_pair * UNIT_PAIR + j
                units = slice(unit_tile * P, (unit_tile + 1) * P)
                sums = psum.tile([P, BANK], F32, tag="bank", name="sums_by_unit")
                for operand in range(OPERANDS):
                    for g in range(PASSES):
                        nc.tensor.matmul_mx(
                            out=sums[:],
                            lhsT=w_codes[block][:, operand, g, units].bitcast(FP8X4),
                            lhsT_scale=w_scales[block][:, operand, g, units],
                            rhs=act_codes[:, operand, g, rows].bitcast(FP8X4),
                            rhs_scale=act_scales[:, operand, g, rows],
                            start=(operand == 0 and g == 0),
                            stop=(operand == OPERANDS - 1 and g == PASSES - 1),
                        )
                column = half * UNIT_TILES + unit_tile
                values = work.tile([P, GROUP, P], F32, tag="g_by_unit", bufs=2 * UNIT_PAIR)
                nc.scalar.activation(
                    out=values[:].rearrange("p i r -> p (i r)"),
                    in_=sums[:],
                    func=TANH,
                    bias=bg_columns[:, column : column + 1],
                )
                g_by_unit[(g_round, j)] = values

        def g_finish(g_round, tiles=(0, 1)):
            step, unit_pair = divmod(g_round, UNIT_TILES // UNIT_PAIR)
            half, group = divmod(step, GROUPS)
            flipped = {}
            for j in tiles:
                g_by_row = psum.tile([P, GROUP, P], F32, tag="bank", name="g_by_row")
                for i in range(GROUP):
                    nc.tensor.transpose(g_by_row[:, i, :], g_by_unit[(g_round, j)][:, i, :], identity[:])
                flipped[j] = g_by_row
            width = len(tiles) * P
            result = work.tile([P, GROUP, UNIT_PAIR * P], F32, tag="result", bufs=3)
            first = (unit_pair * UNIT_PAIR + tiles[0]) * P
            for n_th, j in enumerate(tiles):
                units = slice(half * BANK + first + n_th * P, half * BANK + first + (n_th + 1) * P)
                nc.vector.scalar_tensor_tensor(
                    out=result[:, :, n_th * P : (n_th + 1) * P],
                    in0=flipped[j][:],
                    scalar=1.0,
                    in1=h_rows[group][:, :, units],
                    op0=ALU.subtract,
                    op1=ALU.mult,
                )
            nc.vector.tensor_tensor(
                out=result[:, :, 0:width],
                in0=z_times_s[(half, group)][:, :, first : first + width],
                in1=result[:, :, 0:width],
                op=ALU.subtract,
            )
            nc.sync.dma_start(
                out=group_rows(out, group)[:, :, half * BANK + first : half * BANK + first + width],
                in_=result[:, :, 0:width],
            )

        prepare_rows(0)
        for matrix in range(OPERANDS):
            regroup_weights(matrix)
        load_pair(h_rows, H, 2)
        load_pair(h_rows, H, 3)
        for matrix in range(OPERANDS):
            quantise_weights(matrix)

        for n in range(ROUNDS + G_LAG + 1):
            if n + 1 < PAIRS:
                prepare_rows(n + 1)
            matrix = n + OPERANDS
            if matrix < MATRICES:
                regroup_weights(matrix)
            if n < ROUNDS:
                z_sums(n)
            if n - G_LAG == ROUNDS - 1:
                g_sums(ROUNDS - 1, (0,))
                g_finish(ROUNDS - 2)
                g_sums(ROUNDS - 1, (1,))
                g_finish(ROUNDS - 1, (0,))
                g_finish(ROUNDS - 1, (1,))
                break
            if 0 <= n - G_LAG < ROUNDS:
                g_sums(n - G_LAG)
            if 0 <= n - 1 < ROUNDS:
                z_product(n - 1)
            if 0 <= n - G_LAG - 1 < ROUNDS:
                g_finish(n - G_LAG - 1)
            if matrix < MATRICES:
                quantise_weights(matrix)
